import numpy as np
import ml_dtypes


def mxq(x, axis, fmt="e4m3"):
    dtype, down = {"e4m3": (ml_dtypes.float8_e4m3fn, 7), "e5m2": (ml_dtypes.float8_e5m2, 14)}[fmt]
    v = np.moveaxis(np.asarray(x, np.float32).astype(ml_dtypes.bfloat16).astype(np.float64), axis, -1)
    blocks = v.reshape(v.shape[:-1] + (-1, 32))
    amax = np.abs(blocks).max(-1, keepdims=True)
    byte = np.maximum(np.where(amax > 0, np.frexp(amax)[1] - 1 + 127, 0) - down, 1)
    scale = np.exp2(byte - 127.0)
    codes = (blocks / scale).astype(np.float32).astype(dtype).astype(np.float64)
    return np.moveaxis((codes * scale).reshape(v.shape), -1, axis)


WIDE = False


def mx_kscale(k):
    if not WIDE:
        return np.ones(k)
    levels = np.array([10, -10, 5, -5, 0])
    a = np.random.permutation(np.resize(levels, k // 512 * 4)).reshape(k // 512, 4)
    idx = np.arange(k)
    return np.exp2(a[idx // 512, idx % 128 // 32])


BF16 = ml_dtypes.bfloat16


def bf(x):
    return np.asarray(x, np.float32).astype(BF16)


def f64(x):
    return np.asarray(x).astype(np.float64)


B, D, L = 512, 2048, 4


def relu(v):
    return np.maximum(v, 0.0)


def setup_inputs():
    s = mx_kscale(D)
    return {"h_prev": bf(relu(np.random.standard_normal((B, D))) * s),
            "x": bf(np.random.standard_normal((B, D)) * 1.5 / np.sqrt(np.sqrt(D))),
            "w_last": bf(np.random.standard_normal((D, D)) * 2.0 / np.sqrt(D) / s[None, :]),
            "b_last": bf(np.random.standard_normal(D) * 0.2),
            "w_out": bf(np.random.standard_normal((D, D)) / np.sqrt(D)),
            "b_out": bf(np.random.standard_normal(D) * 0.2)}


def reference(h_prev, x, w_last, b_last, w_out, b_out):
    xf = f64(x)
    interactions = relu(xf * xf.sum(axis=1, keepdims=True))
    h = relu((mxq(f64(h_prev), 1, "e4m3") @ mxq(f64(w_last), 1, "e4m3").T) + f64(b_last))
    z = (h + interactions) * 0.5
    return (mxq(z, 1, "e4m3") @ mxq(f64(w_out), 1, "e4m3").T) + f64(b_out)

@@ -1,0 +1,215 @@
+from contextlib import ExitStack
+
+import concourse.mybir as mybir
+from concourse.masks import make_identity
+
+F32 = mybir.dt.float32
+BF16 = mybir.dt.bfloat16
+I32 = mybir.dt.int32
+U32 = mybir.dt.uint32
+U8 = mybir.dt.uint8
+FP8X4 = mybir.dt.float8_e4m3fn_x4
+ALU = mybir.AluOpType
+ACT = mybir.ActivationFunctionType
+
+P = 128
+B = 512
+D = 2048
+K_PASS = 4 * P
+PASSES = D // K_PASS
+CHUNK = 512
+SLABS = CHUNK // P
+HALF = CHUNK // 2
+B_TILES = B // P
+W_CHUNKS = D // CHUNK
+
+FLOPS = 2 * 2 * B * D * D
+
+
+def tile_deepfm_pa_kernel(tc, h_prev, x, w_last, b_last, w_out, b_out, out):
+    nc = tc.nc
+    with ExitStack() as ctx:
+        const = ctx.enter_context(tc.tile_pool(name="const", bufs=1))
+        slab_pool = ctx.enter_context(tc.tile_pool(name="slabs", bufs=3 * SLABS))
+        stage = ctx.enter_context(tc.tile_pool(name="stage", bufs=6))
+        packed_pool = ctx.enter_context(tc.tile_pool(name="packed", bufs=2))
+        work = ctx.enter_context(tc.tile_pool(name="work", bufs=4))
+        flip_banks = ctx.enter_context(tc.psum_pool(name="flip_banks", bufs=4))
+        acc_banks = ctx.enter_context(tc.psum_pool(name="acc_banks", bufs=4))
+        ctx.enter_context(tc.manual_schedule())
+
+        def load_chunk(matrix, c):
+            slabs = []
+            for s in range(SLABS):
+                slab = slab_pool.tile([P, D], BF16)
+                first = c * CHUNK + s * P
+                nc.sync.dma_start(out=slab[:], in_=matrix[first : first + P, :])
+                slabs.append(slab)
+            return slabs
+
+        def new_packed(pool, label):
+            codes = pool.tile([P, PASSES, CHUNK], U32, align_bytes=64, name=label + "_codes")
+            scales = pool.tile([P, PASSES, CHUNK], U8, align_bytes=64, name=label + "_scales")
+            return codes, scales
+
+        def pack_half(slabs, half, packed, vector_helps):
+            codes, scales = packed
+            rows = slice(half * HALF, (half + 1) * HALF)
+            pair = [slabs[2 * half + s][:].bitcast(F32) for s in range(2)]
+
+            def quantise(g, grouped):
+                nc.vector.quantize_mx(
+                    out=codes[:, g, rows].bitcast(FP8X4),
+                    scales=scales[:, g, rows],
+                    in_=grouped[:].rearrange("p s r u -> p (s r u)").bitcast(BF16),
+                )
+
+            copied = []
+            for g in range(PASSES):
+                flipped = flip_banks.tile([P, 2, 2, P], F32)
+                for s in range(2):
+                    for u in range(2):
+                        first = (2 * g + u) * P
+                        nc.tensor.transpose(
+                            flipped[:, s, u, :], pair[s][:, first : first + P], ident[:]
+                        )
+                grouped = stage.tile([P, 2, P, 2], F32, align_bytes=64)
+                side_by_side = flipped[:].rearrange("p s u r -> p s r u")
+                if vector_helps and g % 2 == 1:
+                    nc.vector.tensor_copy(out=grouped[:], in_=side_by_side)
+                else:
+                    nc.scalar.copy(out=grouped[:], in_=side_by_side)
+                copied.append(grouped)
+                if g > 0:
+                    quantise(g - 1, copied[g - 1])
+            quantise(PASSES - 1, copied[PASSES - 1])
+
+        def multiply(act, weights, bt):
+            act_codes, act_scales = act
+            w_codes, w_scales = weights
+            rows = slice(bt * P, (bt + 1) * P)
+            acc = acc_banks.tile([P, CHUNK], F32)
+            for g in range(PASSES):
+                nc.tensor.matmul_mx(
+                    out=acc[:],
+                    lhsT=act_codes[:, g, rows].bitcast(FP8X4),
+                    lhsT_scale=act_scales[:, g, rows],
+                    rhs=w_codes[:, g, :].bitcast(FP8X4),
+                    rhs_scale=w_scales[:, g, :],
+                    start=(g == 0),
+                    stop=(g == PASSES - 1),
+                )
+            return acc
+
+        def load_bias_row(bias, label):
+            row = const.tile([P, D], BF16, name=label + "_row")
+            nc.vector.memset(row[:].bitcast(I32), 0)
+            nc.sync.dma_start(out=row[0:1, :], in_=bias.rearrange("(o d) -> o d", o=1))
+            return row
+
+        def spread_bias(row, factor, label):
+            spread = const.tile([P, D], F32, name=label + "_spread")
+            for c in range(W_CHUNKS):
+                cols = slice(c * CHUNK, (c + 1) * CHUNK)
+                acc = acc_banks.tile([P, CHUNK], F32)
+                nc.tensor.matmul(acc[:], lhsT=ones[:], rhs=row[:, cols], start=True, stop=True)
+                nc.vector.tensor_scalar_mul(out=spread[:, cols], in0=acc[:], scalar1=factor)
+            return spread
+
+        b_last_row = load_bias_row(b_last, "b_last")
+        ident = const.tile([P, P], F32)
+        make_identity(nc, ident[:])
+        ones = const.tile([P, P], BF16)
+        nc.vector.memset(ones[:], 1.0)
+
+        matrices = [w_last] * W_CHUNKS + [w_out] * W_CHUNKS
+        n_chunks = len(matrices)
+        w_slabs = {}
+        w_packed = {}
+
+        def load_weights(i):
+            if i < n_chunks:
+                w_slabs[i] = load_chunk(matrices[i], i % W_CHUNKS)
+
+        def pack_weights_half(i, half, vector_helps):
+            if i < n_chunks:
+                if half == 0:
+                    w_packed[i] = new_packed(packed_pool, "w")
+                pack_half(w_slabs[i], half, w_packed[i], vector_helps)
+
+        h_slabs = load_chunk(h_prev, 0)
+        load_weights(0)
+        x_slabs = []
+        for bt in range(B_TILES):
+            x_slab = const.tile([P, D], BF16, name="x_slab%d" % bt)
+            nc.sync.dma_start(out=x_slab[:], in_=x[bt * P : (bt + 1) * P, :])
+            x_slabs.append(x_slab)
+        load_weights(1)
+        b_out_row = load_bias_row(b_out, "b_out")
+
+        h_packed = new_packed(const, "h")
+        for half in range(2):
+            pack_half(h_slabs, half, h_packed, True)
+        load_weights(2)
+        half_b_last = spread_bias(b_last_row, 0.5, "b_last")
+        for half in range(2):
+            pack_weights_half(0, half, True)
+
+        half_sum = const.tile([P, B_TILES], F32)
+        halved = const.tile([P, D], BF16)
+        for bt in range(B_TILES):
+            nc.vector.tensor_scalar(
+                out=halved[:],
+                in0=x_slabs[bt][:],
+                scalar1=0.5,
+                scalar2=None,
+                op0=ALU.mult,
+                op1=ALU.add,
+                accum_out=half_sum[:, bt : bt + 1],
+            )
+
+        z_slabs = []
+        for bt in range(B_TILES):
+            z_slab = const.tile([P, D], BF16, name="z_slab%d" % bt)
+            z_slabs.append(z_slab)
+
+        def finish_hidden(acc, bt, c):
+            cols = slice(c * CHUNK, (c + 1) * CHUNK)
+            pre = work.tile([P, CHUNK], F32)
+            nc.vector.scalar_tensor_tensor(
+                out=pre[:], in0=acc[:], scalar=0.5, in1=half_b_last[:, cols],
+                op0=ALU.mult, op1=ALU.add,
+            )
+            inter = work.tile([P, CHUNK], F32)
+            nc.scalar.activation(
+                out=inter[:], in_=x_slabs[bt][:, cols], func=ACT.Relu,
+                scale=half_sum[:, bt : bt + 1],
+            )
+            nc.vector.scalar_tensor_tensor(
+                out=z_slabs[bt][:, cols], in0=pre[:], scalar=0.0, in1=inter[:],
+                op0=ALU.max, op1=ALU.add,
+            )
+
+        def finish_output(acc, bt, c):
+            cols = slice(c * CHUNK, (c + 1) * CHUNK)
+            result = work.tile([P, CHUNK], F32)
+            nc.vector.tensor_tensor(out=result[:], in0=acc[:], in1=b_out_all[:, cols], op=ALU.add)
+            nc.sync.dma_start(out=out[bt * P : (bt + 1) * P, cols], in_=result[:])
+
+        def layer(first, act, finish):
+            for i in range(first, first + W_CHUNKS):
+                load_weights(i + 3)
+                for half in range(2):
+                    for bt in (2 * half, 2 * half + 1):
+                        acc = multiply(act, w_packed[i], bt)
+                        finish(acc, bt, i - first)
+                    pack_weights_half(i + 1, half, False)
+
+        layer(0, h_packed, finish_hidden)
+
+        z_packed = new_packed(const, "z")
+        pack_half(z_slabs, 0, z_packed, True)
+        b_out_all = spread_bias(b_out_row, 1.0, "b_out")
+        pack_half(z_slabs, 1, z_packed, True)
+
+        layer(W_CHUNKS, z_packed, finish_output)

@@ -22,6 +22,7 @@ SLABS = CHUNK // P
 HALF = CHUNK // 2
 B_TILES = B // P
 W_CHUNKS = D // CHUNK
+PACK_LEAD = 3
 
 FLOPS = 2 * 2 * B * D * D
 
@@ -32,7 +33,7 @@ def tile_deepfm_pa_kernel(tc, h_prev, x, w_last, b_last, w_out, b_out, out):
         const = ctx.enter_context(tc.tile_pool(name="const", bufs=1))
         slab_pool = ctx.enter_context(tc.tile_pool(name="slabs", bufs=3 * SLABS))
         stage = ctx.enter_context(tc.tile_pool(name="stage", bufs=6))
-        packed_pool = ctx.enter_context(tc.tile_pool(name="packed", bufs=2))
+        packed_pool = ctx.enter_context(tc.tile_pool(name="packed", bufs=3))
         work = ctx.enter_context(tc.tile_pool(name="work", bufs=4))
         flip_banks = ctx.enter_context(tc.psum_pool(name="flip_banks", bufs=4))
         acc_banks = ctx.enter_context(tc.psum_pool(name="acc_banks", bufs=4))
@@ -52,7 +53,7 @@ def tile_deepfm_pa_kernel(tc, h_prev, x, w_last, b_last, w_out, b_out, out):
             scales = pool.tile([P, PASSES, CHUNK], U8, align_bytes=64, name=label + "_scales")
             return codes, scales
 
-        def pack_half(slabs, half, packed, vector_helps):
+        def pack_half(slabs, half, packed):
             codes, scales = packed
             rows = slice(half * HALF, (half + 1) * HALF)
             pair = [slabs[2 * half + s][:].bitcast(F32) for s in range(2)]
@@ -74,11 +75,7 @@ def tile_deepfm_pa_kernel(tc, h_prev, x, w_last, b_last, w_out, b_out, out):
                             flipped[:, s, u, :], pair[s][:, first : first + P], ident[:]
                         )
                 grouped = stage.tile([P, 2, P, 2], F32, align_bytes=64)
-                side_by_side = flipped[:].rearrange("p s u r -> p s r u")
-                if vector_helps and g % 2 == 1:
-                    nc.vector.tensor_copy(out=grouped[:], in_=side_by_side)
-                else:
-                    nc.scalar.copy(out=grouped[:], in_=side_by_side)
+                nc.scalar.copy(out=grouped[:], in_=flipped[:].rearrange("p s u r -> p s r u"))
                 copied.append(grouped)
                 if g > 0:
                     quantise(g - 1, copied[g - 1])
@@ -104,7 +101,7 @@ def tile_deepfm_pa_kernel(tc, h_prev, x, w_last, b_last, w_out, b_out, out):
         def load_bias_row(bias, label):
             row = const.tile([P, D], BF16, name=label + "_row")
             nc.vector.memset(row[:].bitcast(I32), 0)
-            nc.sync.dma_start(out=row[0:1, :], in_=bias.rearrange("(o d) -> o d", o=1))
+            nc.scalar.dma_start(out=row[0:1, :], in_=bias.rearrange("(o d) -> o d", o=1))
             return row
 
         def spread_bias(row, factor, label):
@@ -117,6 +114,7 @@ def tile_deepfm_pa_kernel(tc, h_prev, x, w_last, b_last, w_out, b_out, out):
             return spread
 
         b_last_row = load_bias_row(b_last, "b_last")
+        b_out_row = load_bias_row(b_out, "b_out")
         ident = const.tile([P, P], F32)
         make_identity(nc, ident[:])
         ones = const.tile([P, P], BF16)
@@ -131,11 +129,15 @@ def tile_deepfm_pa_kernel(tc, h_prev, x, w_last, b_last, w_out, b_out, out):
             if i < n_chunks:
                 w_slabs[i] = load_chunk(matrices[i], i % W_CHUNKS)
 
-        def pack_weights_half(i, half, vector_helps):
-            if i < n_chunks:
+        halves_packed = []
+
+        def pack_weights_up_to(last):
+            for n in range(len(halves_packed), min(last + 1, 2 * n_chunks)):
+                i, half = divmod(n, 2)
                 if half == 0:
                     w_packed[i] = new_packed(packed_pool, "w")
-                pack_half(w_slabs[i], half, w_packed[i], vector_helps)
+                pack_half(w_slabs[i], half, w_packed[i])
+                halves_packed.append(n)
 
         h_slabs = load_chunk(h_prev, 0)
         load_weights(0)
@@ -145,15 +147,13 @@ def tile_deepfm_pa_kernel(tc, h_prev, x, w_last, b_last, w_out, b_out, out):
             nc.sync.dma_start(out=x_slab[:], in_=x[bt * P : (bt + 1) * P, :])
             x_slabs.append(x_slab)
         load_weights(1)
-        b_out_row = load_bias_row(b_out, "b_out")
 
         h_packed = new_packed(const, "h")
         for half in range(2):
-            pack_half(h_slabs, half, h_packed, True)
+            pack_half(h_slabs, half, h_packed)
         load_weights(2)
         half_b_last = spread_bias(b_last_row, 0.5, "b_last")
-        for half in range(2):
-            pack_weights_half(0, half, True)
+        pack_weights_up_to(1)
 
         half_sum = const.tile([P, B_TILES], F32)
         halved = const.tile([P, D], BF16)
@@ -203,13 +203,13 @@ def tile_deepfm_pa_kernel(tc, h_prev, x, w_last, b_last, w_out, b_out, out):
                     for bt in (2 * half, 2 * half + 1):
                         acc = multiply(act, w_packed[i], bt)
                         finish(acc, bt, i - first)
-                    pack_weights_half(i + 1, half, False)
+                    pack_weights_up_to(2 * i + half + PACK_LEAD)
 
         layer(0, h_packed, finish_hidden)
 
         z_packed = new_packed(const, "z")
-        pack_half(z_slabs, 0, z_packed, True)
+        pack_half(z_slabs, 0, z_packed)
         b_out_all = spread_bias(b_out_row, 1.0, "b_out")
-        pack_half(z_slabs, 1, z_packed, True)
+        pack_half(z_slabs, 1, z_packed)
 
         layer(W_CHUNKS, z_packed, finish_output)

@@ -114,7 +114,6 @@ def tile_deepfm_pa_kernel(tc, h_prev, x, w_last, b_last, w_out, b_out, out):
             return spread
 
         b_last_row = load_bias_row(b_last, "b_last")
-        b_out_row = load_bias_row(b_out, "b_out")
         ident = const.tile([P, P], F32)
         make_identity(nc, ident[:])
         ones = const.tile([P, P], BF16)
@@ -203,13 +202,17 @@ def tile_deepfm_pa_kernel(tc, h_prev, x, w_last, b_last, w_out, b_out, out):
                     for bt in (2 * half, 2 * half + 1):
                         acc = multiply(act, w_packed[i], bt)
                         finish(acc, bt, i - first)
-                    pack_weights_up_to(2 * i + half + PACK_LEAD)
+                    step = 2 * i + half
+                    if step < 2 * (first + W_CHUNKS) - 1:
+                        pack_weights_up_to(step + PACK_LEAD)
 
         layer(0, h_packed, finish_hidden)
 
+        b_out_all = const.tile([P, D], BF16)
+        nc.sync.dma_start(out=b_out_all[:], in_=b_out.partition_broadcast(P))
+
         z_packed = new_packed(const, "z")
-        pack_half(z_slabs, 0, z_packed)
-        b_out_all = spread_bias(b_out_row, 1.0, "b_out")
-        pack_half(z_slabs, 1, z_packed)
+        for half in range(2):
+            pack_half(z_slabs, half, z_packed)
 
         layer(W_CHUNKS, z_packed, finish_output)

@@ -114,6 +114,7 @@ def tile_deepfm_pa_kernel(tc, h_prev, x, w_last, b_last, w_out, b_out, out):
             return spread
 
         b_last_row = load_bias_row(b_last, "b_last")
+        b_out_row = load_bias_row(b_out, "b_out")
         ident = const.tile([P, P], F32)
         make_identity(nc, ident[:])
         ones = const.tile([P, P], BF16)
@@ -172,47 +173,49 @@ def tile_deepfm_pa_kernel(tc, h_prev, x, w_last, b_last, w_out, b_out, out):
             z_slab = const.tile([P, D], BF16, name="z_slab%d" % bt)
             z_slabs.append(z_slab)
 
-        def finish_hidden(acc, bt, c):
+        def finish_hidden(sums, c):
             cols = slice(c * CHUNK, (c + 1) * CHUNK)
-            pre = work.tile([P, CHUNK], F32)
-            nc.vector.scalar_tensor_tensor(
-                out=pre[:], in0=acc[:], scalar=0.5, in1=half_b_last[:, cols],
-                op0=ALU.mult, op1=ALU.add,
-            )
-            inter = work.tile([P, CHUNK], F32)
-            nc.scalar.activation(
-                out=inter[:], in_=x_slabs[bt][:, cols], func=ACT.Relu,
-                scale=half_sum[:, bt : bt + 1],
-            )
-            nc.vector.scalar_tensor_tensor(
-                out=z_slabs[bt][:, cols], in0=pre[:], scalar=0.0, in1=inter[:],
-                op0=ALU.max, op1=ALU.add,
-            )
+            waiting = []
+            for bt, acc in sums:
+                pre = work.tile([P, CHUNK], F32)
+                nc.vector.scalar_tensor_tensor(
+                    out=pre[:], in0=acc[:], scalar=0.5, in1=half_b_last[:, cols],
+                    op0=ALU.mult, op1=ALU.add,
+                )
+                waiting.append((bt, pre))
+            for bt, pre in waiting:
+                inter = work.tile([P, CHUNK], F32)
+                nc.scalar.activation(
+                    out=inter[:], in_=x_slabs[bt][:, cols], func=ACT.Relu,
+                    scale=half_sum[:, bt : bt + 1],
+                )
+                nc.vector.scalar_tensor_tensor(
+                    out=z_slabs[bt][:, cols], in0=pre[:], scalar=0.0, in1=inter[:],
+                    op0=ALU.max, op1=ALU.add,
+                )
 
-        def finish_output(acc, bt, c):
+        def finish_output(sums, c):
             cols = slice(c * CHUNK, (c + 1) * CHUNK)
-            result = work.tile([P, CHUNK], F32)
-            nc.vector.tensor_tensor(out=result[:], in0=acc[:], in1=b_out_all[:, cols], op=ALU.add)
-            nc.sync.dma_start(out=out[bt * P : (bt + 1) * P, cols], in_=result[:])
+            for bt, acc in sums:
+                result = work.tile([P, CHUNK], F32)
+                nc.vector.tensor_tensor(
+                    out=result[:], in0=acc[:], in1=b_out_all[:, cols], op=ALU.add
+                )
+                nc.sync.dma_start(out=out[bt * P : (bt + 1) * P, cols], in_=result[:])
 
         def layer(first, act, finish):
             for i in range(first, first + W_CHUNKS):
                 load_weights(i + 3)
                 for half in range(2):
-                    for bt in (2 * half, 2 * half + 1):
-                        acc = multiply(act, w_packed[i], bt)
-                        finish(acc, bt, i - first)
-                    step = 2 * i + half
-                    if step < 2 * (first + W_CHUNKS) - 1:
-                        pack_weights_up_to(step + PACK_LEAD)
+                    sums = [(bt, multiply(act, w_packed[i], bt)) for bt in (2 * half, 2 * half + 1)]
+                    finish(sums, i - first)
+                    pack_weights_up_to(2 * i + half + PACK_LEAD)
 
         layer(0, h_packed, finish_hidden)
 
-        b_out_all = const.tile([P, D], BF16)
-        nc.sync.dma_start(out=b_out_all[:], in_=b_out.partition_broadcast(P))
-
         z_packed = new_packed(const, "z")
-        for half in range(2):
-            pack_half(z_slabs, half, z_packed)
+        pack_half(z_slabs, 0, z_packed)
+        b_out_all = spread_bias(b_out_row, 1.0, "b_out")
+        pack_half(z_slabs, 1, z_packed)
 
         layer(W_CHUNKS, z_packed, finish_output)

@@ -49,8 +49,8 @@ def tile_deepfm_pa_kernel(tc, h_prev, x, w_last, b_last, w_out, b_out, out):
             return slabs
 
         def new_packed(pool, label):
-            codes = pool.tile([P, PASSES, CHUNK], U32, align_bytes=64, name=label + "_codes")
-            scales = pool.tile([P, PASSES, CHUNK], U8, align_bytes=64, name=label + "_scales")
+            codes = pool.tile([P, PASSES, CHUNK], U32, align_bytes=256, name=label + "_codes")
+            scales = pool.tile([P, PASSES, CHUNK], U8, align_bytes=256, name=label + "_scales")
             return codes, scales
 
         def pack_half(slabs, half, packed):
@@ -74,7 +74,7 @@ def tile_deepfm_pa_kernel(tc, h_prev, x, w_last, b_last, w_out, b_out, out):
                         nc.tensor.transpose(
                             flipped[:, s, u, :], pair[s][:, first : first + P], ident[:]
                         )
-                grouped = stage.tile([P, 2, P, 2], F32, align_bytes=64)
+                grouped = stage.tile([P, 2, P, 2], F32, align_bytes=256)
                 nc.scalar.copy(out=grouped[:], in_=flipped[:].rearrange("p s u r -> p s r u"))
                 copied.append(grouped)
                 if g > 0:

from contextlib import ExitStack

import concourse.mybir as mybir
from concourse.masks import make_identity

F32 = mybir.dt.float32
BF16 = mybir.dt.bfloat16
I32 = mybir.dt.int32
U32 = mybir.dt.uint32
U8 = mybir.dt.uint8
FP8X4 = mybir.dt.float8_e4m3fn_x4
ALU = mybir.AluOpType
ACT = mybir.ActivationFunctionType

P = 128
B = 512
D = 2048
K_PASS = 4 * P
PASSES = D // K_PASS
CHUNK = 512
SLABS = CHUNK // P
HALF = CHUNK // 2
B_TILES = B // P
W_CHUNKS = D // CHUNK
PACK_LEAD = 3

FLOPS = 2 * 2 * B * D * D


def tile_deepfm_pa_kernel(tc, h_prev, x, w_last, b_last, w_out, b_out, out):
    nc = tc.nc
    with ExitStack() as ctx:
        const = ctx.enter_context(tc.tile_pool(name="const", bufs=1))
        slab_pool = ctx.enter_context(tc.tile_pool(name="slabs", bufs=3 * SLABS))
        stage = ctx.enter_context(tc.tile_pool(name="stage", bufs=6))
        packed_pool = ctx.enter_context(tc.tile_pool(name="packed", bufs=3))
        work = ctx.enter_context(tc.tile_pool(name="work", bufs=4))
        flip_banks = ctx.enter_context(tc.psum_pool(name="flip_banks", bufs=4))
        acc_banks = ctx.enter_context(tc.psum_pool(name="acc_banks", bufs=4))
        ctx.enter_context(tc.manual_schedule())

        def load_chunk(matrix, c):
            slabs = []
            for s in range(SLABS):
                slab = slab_pool.tile([P, D], BF16)
                first = c * CHUNK + s * P
                nc.sync.dma_start(out=slab[:], in_=matrix[first : first + P, :])
                slabs.append(slab)
            return slabs

        def new_packed(pool, label):
            codes = pool.tile([P, PASSES, CHUNK], U32, align_bytes=256, name=label + "_codes")
            scales = pool.tile([P, PASSES, CHUNK], U8, align_bytes=256, name=label + "_scales")
            return codes, scales

        def pack_half(slabs, half, packed):
            codes, scales = packed
            rows = slice(half * HALF, (half + 1) * HALF)
            pair = [slabs[2 * half + s][:].bitcast(F32) for s in range(2)]

            def quantise(g, grouped):
                nc.vector.quantize_mx(
                    out=codes[:, g, rows].bitcast(FP8X4),
                    scales=scales[:, g, rows],
                    in_=grouped[:].rearrange("p s r u -> p (s r u)").bitcast(BF16),
                )

            copied = []
            for g in range(PASSES):
                flipped = flip_banks.tile([P, 2, 2, P], F32)
                for s in range(2):
                    for u in range(2):
                        first = (2 * g + u) * P
                        nc.tensor.transpose(
                            flipped[:, s, u, :], pair[s][:, first : first + P], ident[:]
                        )
                grouped = stage.tile([P, 2, P, 2], F32, align_bytes=256)
                nc.scalar.copy(out=grouped[:], in_=flipped[:].rearrange("p s u r -> p s r u"))
                copied.append(grouped)
                if g > 0:
                    quantise(g - 1, copied[g - 1])
            quantise(PASSES - 1, copied[PASSES - 1])

        def multiply(act, weights, bt):
            act_codes, act_scales = act
            w_codes, w_scales = weights
            rows = slice(bt * P, (bt + 1) * P)
            acc = acc_banks.tile([P, CHUNK], F32)
            for g in range(PASSES):
                nc.tensor.matmul_mx(
                    out=acc[:],
                    lhsT=act_codes[:, g, rows].bitcast(FP8X4),
                    lhsT_scale=act_scales[:, g, rows],
                    rhs=w_codes[:, g, :].bitcast(FP8X4),
                    rhs_scale=w_scales[:, g, :],
                    start=(g == 0),
                    stop=(g == PASSES - 1),
                )
            return acc

        def load_bias_row(bias, label):
            row = const.tile([P, D], BF16, name=label + "_row")
            nc.vector.memset(row[:].bitcast(I32), 0)
            nc.scalar.dma_start(out=row[0:1, :], in_=bias.rearrange("(o d) -> o d", o=1))
            return row

        def spread_bias(row, factor, label):
            spread = const.tile([P, D], F32, name=label + "_spread")
            for c in range(W_CHUNKS):
                cols = slice(c * CHUNK, (c + 1) * CHUNK)
                acc = acc_banks.tile([P, CHUNK], F32)
                nc.tensor.matmul(acc[:], lhsT=ones[:], rhs=row[:, cols], start=True, stop=True)
                nc.vector.tensor_scalar_mul(out=spread[:, cols], in0=acc[:], scalar1=factor)
            return spread

        b_last_row = load_bias_row(b_last, "b_last")
        b_out_row = load_bias_row(b_out, "b_out")
        ident = const.tile([P, P], F32)
        make_identity(nc, ident[:])
        ones = const.tile([P, P], BF16)
        nc.vector.memset(ones[:], 1.0)

        matrices = [w_last] * W_CHUNKS + [w_out] * W_CHUNKS
        n_chunks = len(matrices)
        w_slabs = {}
        w_packed = {}

        def load_weights(i):
            if i < n_chunks:
                w_slabs[i] = load_chunk(matrices[i], i % W_CHUNKS)

        halves_packed = []

        def pack_weights_up_to(last):
            for n in range(len(halves_packed), min(last + 1, 2 * n_chunks)):
                i, half = divmod(n, 2)
                if half == 0:
                    w_packed[i] = new_packed(packed_pool, "w")
                pack_half(w_slabs[i], half, w_packed[i])
                halves_packed.append(n)

        h_slabs = load_chunk(h_prev, 0)
        load_weights(0)
        x_slabs = []
        for bt in range(B_TILES):
            x_slab = const.tile([P, D], BF16, name="x_slab%d" % bt)
            nc.sync.dma_start(out=x_slab[:], in_=x[bt * P : (bt + 1) * P, :])
            x_slabs.append(x_slab)
        load_weights(1)

        h_packed = new_packed(const, "h")
        for half in range(2):
            pack_half(h_slabs, half, h_packed)
        load_weights(2)
        half_b_last = spread_bias(b_last_row, 0.5, "b_last")
        pack_weights_up_to(1)

        half_sum = const.tile([P, B_TILES], F32)
        halved = const.tile([P, D], BF16)
        for bt in range(B_TILES):
            nc.vector.tensor_scalar(
                out=halved[:],
                in0=x_slabs[bt][:],
                scalar1=0.5,
                scalar2=None,
                op0=ALU.mult,
                op1=ALU.add,
                accum_out=half_sum[:, bt : bt + 1],
            )

        z_slabs = []
        for bt in range(B_TILES):
            z_slab = const.tile([P, D], BF16, name="z_slab%d" % bt)
            z_slabs.append(z_slab)

        def finish_hidden(sums, c):
            cols = slice(c * CHUNK, (c + 1) * CHUNK)
            waiting = []
            for bt, acc in sums:
                pre = work.tile([P, CHUNK], F32)
                nc.vector.scalar_tensor_tensor(
                    out=pre[:], in0=acc[:], scalar=0.5, in1=half_b_last[:, cols],
                    op0=ALU.mult, op1=ALU.add,
                )
                waiting.append((bt, pre))
            for bt, pre in waiting:
                inter = work.tile([P, CHUNK], F32)
                nc.scalar.activation(
                    out=inter[:], in_=x_slabs[bt][:, cols], func=ACT.Relu,
                    scale=half_sum[:, bt : bt + 1],
                )
                nc.vector.scalar_tensor_tensor(
                    out=z_slabs[bt][:, cols], in0=pre[:], scalar=0.0, in1=inter[:],
                    op0=ALU.max, op1=ALU.add,
                )

        def finish_output(sums, c):
            cols = slice(c * CHUNK, (c + 1) * CHUNK)
            for bt, acc in sums:
                result = work.tile([P, CHUNK], F32)
                nc.vector.tensor_tensor(
                    out=result[:], in0=acc[:], in1=b_out_all[:, cols], op=ALU.add
                )
                nc.sync.dma_start(out=out[bt * P : (bt + 1) * P, cols], in_=result[:])

        def layer(first, act, finish):
            for i in range(first, first + W_CHUNKS):
                load_weights(i + 3)
                for half in range(2):
                    sums = [(bt, multiply(act, w_packed[i], bt)) for bt in (2 * half, 2 * half + 1)]
                    finish(sums, i - first)
                    pack_weights_up_to(2 * i + half + PACK_LEAD)

        layer(0, h_packed, finish_hidden)

        z_packed = new_packed(const, "z")
        pack_half(z_slabs, 0, z_packed)
        b_out_all = spread_bias(b_out_row, 1.0, "b_out")
        pack_half(z_slabs, 1, z_packed)

        layer(W_CHUNKS, z_packed, finish_output)
